import numpy as np
import ml_dtypes


def mxq(x, axis, fmt="e4m3"):
    dtype, down = {"e4m3": (ml_dtypes.float8_e4m3fn, 7), "e5m2": (ml_dtypes.float8_e5m2, 14)}[fmt]
    v = np.moveaxis(np.asarray(x, np.float32).astype(ml_dtypes.bfloat16).astype(np.float64), axis, -1)
    blocks = v.reshape(v.shape[:-1] + (-1, 32))
    amax = np.abs(blocks).max(-1, keepdims=True)
    byte = np.maximum(np.where(amax > 0, np.frexp(amax)[1] - 1 + 127, 0) - down, 1)
    scale = np.exp2(byte - 127.0)
    codes = (blocks / scale).astype(np.float32).astype(dtype).astype(np.float64)
    return np.moveaxis((codes * scale).reshape(v.shape), -1, axis)


WIDE = False


def mx_kscale(k):
    if not WIDE:
        return np.ones(k)
    levels = np.array([10, -10, 5, -5, 0])
    a = np.random.permutation(np.resize(levels, k // 512 * 4)).reshape(k // 512, 4)
    idx = np.arange(k)
    return np.exp2(a[idx // 512, idx % 128 // 32])


BF16 = ml_dtypes.bfloat16


def bf(x):
    return np.asarray(x, np.float32).astype(BF16)


def f64(x):
    return np.asarray(x).astype(np.float64)


B, X, N, OS = 8192, 512, 640, 128
H = N - OS


def setup_inputs():
    s, t = mx_kscale(X), mx_kscale(H)
    std0 = np.sqrt(2.0 / X)
    std1 = np.sqrt(2.0 / (X + H))
    row_scale = np.concatenate([std0 * t, np.full(OS, std1)])
    bias_scale = np.concatenate([t, np.ones(OS)])
    return {"x": bf(np.random.standard_normal((B, X)) * s),
            "w0": bf(np.random.standard_normal((N, X)) * row_scale[:, None] / s),
            "w1": bf(np.random.standard_normal((OS, H)) * std1 / t),
            "biases": bf(np.random.random(N) * bias_scale)}


def reference(x, w0, w1, biases):
    n = w0.shape[0]
    os_ = w1.shape[0]
    z = (mxq(f64(x), 1, "e4m3") @ mxq(f64(w0), 1, "e4m3").T) + f64(biases)
    h = np.maximum(z[:, : n - os_], 0.0)
    return z[:, n - os_:] + (mxq(h, 1, "e4m3") @ mxq(f64(w1), 1, "e4m3").T)

@@ -1,0 +1,246 @@
+from contextlib import ExitStack
+
+import concourse.mybir as mybir
+from concourse.masks import make_identity
+
+BF16 = mybir.dt.bfloat16
+F32 = mybir.dt.float32
+U32 = mybir.dt.uint32
+U8 = mybir.dt.uint8
+FP8X4 = mybir.dt.float8_e4m3fn_x4
+
+P = 128
+PACK = 4
+HALVES = 2
+BATCH = 8192
+INPUTS = 512
+HIDDEN = 512
+OUTS = 128
+ROUND = 512
+TILES = ROUND // P
+ROUNDS = BATCH // ROUND
+W_TILES = 6
+
+OUT_W0 = slice(HIDDEN, HIDDEN + OUTS)
+W1 = slice(HIDDEN + OUTS, HIDDEN + 2 * OUTS)
+
+FLOPS = 2 * BATCH * INPUTS * (HIDDEN + OUTS) + 2 * BATCH * HIDDEN * OUTS
+
+
+def transpose_two_tiles(nc, banks, identity, rows, first):
+    bank = banks.tile([P, 2, HALVES, P], F32, tag="bank")
+    for j in range(2):
+        words = rows[:, first + j, :].bitcast(F32)
+        for u in range(HALVES):
+            nc.tensor.transpose(
+                out=bank[:, j, u, :],
+                in_=words[:, u * P : (u + 1) * P],
+                identity=identity[:],
+            )
+    return bank
+
+
+def words_side_by_side(bank):
+    return bank[:].rearrange("p j u r -> p j r u")
+
+
+def tile_spn_t_kernel(tc, x, w0, w1, biases, out):
+    nc = tc.nc
+    with ExitStack() as stack:
+        stack.enter_context(tc.manual_schedule())
+        keep = stack.enter_context(tc.tile_pool(name="keep", bufs=1))
+        pairs = stack.enter_context(tc.tile_pool(name="pairs", bufs=2))
+        triples = stack.enter_context(tc.tile_pool(name="triples", bufs=3))
+        fours = stack.enter_context(tc.tile_pool(name="fours", bufs=4))
+        transposed_psum = stack.enter_context(tc.psum_pool(name="transposed", bufs=2))
+        hidden_psum = stack.enter_context(tc.psum_pool(name="hidden", bufs=PACK))
+        result_psum = stack.enter_context(tc.psum_pool(name="result", bufs=2))
+
+        w_rows = keep.tile([P, W_TILES, INPUTS], BF16)
+        nc.sync.dma_start(
+            out=w_rows[:, 0:PACK, :].rearrange("m (u e) k -> m u (e k)", u=HALVES),
+            in_=w0[0:HIDDEN, :].rearrange("(u m e) k -> m u (e k)", u=HALVES, e=2),
+        )
+        nc.sync.dma_start(out=w_rows[:, PACK, :], in_=w0[HIDDEN : HIDDEN + OUTS, :])
+        nc.sync.dma_start(out=w_rows[:, PACK + 1, :], in_=w1[:, :])
+        x_rows = []
+        for r in range(ROUNDS):
+            rows = keep.tile([P, TILES, INPUTS], BF16, name="x_rows_%d" % r)
+            nc.sync.dma_start(
+                out=rows[:],
+                in_=x[r * ROUND : (r + 1) * ROUND, :].rearrange("(p j) k -> p j k", j=TILES),
+            )
+            x_rows.append(rows)
+        bias_hidden = keep.tile([P, PACK], BF16)
+        nc.scalar.dma_start(
+            out=bias_hidden[:].rearrange("m (u e) -> m u e", u=HALVES),
+            in_=biases[0:HIDDEN].rearrange("(u m e) -> m u e", u=HALVES, e=2),
+        )
+        bias_out = keep.tile([P, OUTS], BF16)
+        nc.scalar.dma_start(
+            out=bias_out[:], in_=biases[HIDDEN : HIDDEN + OUTS].partition_broadcast(P)
+        )
+
+        identity = keep.tile([P, P], F32)
+        make_identity(nc, identity[:])
+
+        w_grouped = keep.tile([P, W_TILES, P, PACK], BF16, align_bytes=64)
+        w_codes = keep.tile([P, W_TILES * P], U32, align_bytes=64)
+        w_scales = keep.tile([P, W_TILES * P], U8, align_bytes=64)
+        for first in range(0, W_TILES, 2):
+            bank = transpose_two_tiles(nc, hidden_psum, identity, w_rows, first)
+            nc.vector.tensor_copy(
+                out=w_grouped[:, first : first + 2, :, :].bitcast(F32),
+                in_=words_side_by_side(bank),
+            )
+        for first, last in ((0, 4), (4, 6)):
+            columns = slice(first * P, last * P)
+            nc.vector.quantize_mx(
+                out=w_codes[:, columns].bitcast(FP8X4),
+                scales=w_scales[:, columns],
+                in_=w_grouped[:, first:last, :, :].rearrange("p j r t -> p (j r t)"),
+            )
+
+        x_banks = {}
+        x_grouped = {}
+        x_mx = {}
+        h_banks = {}
+        h_planes = {}
+        h_grouped = {}
+        h_mx = {}
+        result_banks = {}
+
+        def transpose_x(r):
+            x_banks[r] = [
+                transpose_two_tiles(nc, transposed_psum, identity, x_rows[r], first)
+                for first in range(0, TILES, 2)
+            ]
+
+        def copy_x_out(r):
+            grouped = pairs.tile([P, TILES, P, PACK], BF16, align_bytes=64, name="x_grouped")
+            for b, bank in enumerate(x_banks[r]):
+                nc.scalar.copy(
+                    out=grouped[:, 2 * b : 2 * b + 2, :, :].bitcast(F32),
+                    in_=words_side_by_side(bank),
+                )
+            x_grouped[r] = grouped
+
+        def quantise_x(r):
+            codes = fours.tile([P, ROUND], U32, align_bytes=64, name="x_codes")
+            scales = fours.tile([P, ROUND], U8, align_bytes=64, name="x_scales")
+            nc.vector.quantize_mx(
+                out=codes[:].bitcast(FP8X4),
+                scales=scales[:],
+                in_=x_grouped[r][:].rearrange("p j r t -> p (j r t)"),
+            )
+            x_mx[r] = (codes, scales)
+
+        def hidden_matmuls(r):
+            codes, scales = x_mx[r]
+            h_banks[r] = []
+            for t in range(PACK):
+                nodes = slice(t * P, (t + 1) * P)
+                bank = hidden_psum.tile([P, ROUND], F32, tag="bank")
+                nc.tensor.matmul_mx(
+                    out=bank[:],
+                    lhsT=w_codes[:, nodes].bitcast(FP8X4),
+                    lhsT_scale=w_scales[:, nodes],
+                    rhs=codes[:].bitcast(FP8X4),
+                    rhs_scale=scales[:],
+                    start=True,
+                    stop=True,
+                )
+                h_banks[r].append(bank)
+
+        def relu_out(r):
+            planes = triples.tile([P, PACK, ROUND], BF16, name="h_planes")
+            for t, bank in enumerate(h_banks[r]):
+                nc.scalar.activation(
+                    out=planes[:, t, :],
+                    in_=bank[:],
+                    func=mybir.ActivationFunctionType.Relu,
+                    bias=bias_hidden[:, t : t + 1],
+                    scale=1.0,
+                )
+            h_planes[r] = planes
+
+        def regroup_h(r):
+            grouped = pairs.tile([P, ROUND, PACK], BF16, align_bytes=64, name="h_grouped")
+            nc.vector.tensor_copy(
+                out=grouped[:].rearrange("p (c i) t -> p c t i", i=4),
+                in_=h_planes[r][:].rearrange("p t (c i) -> p c t i", i=4),
+            )
+            h_grouped[r] = grouped
+
+        def quantise_h(r):
+            codes = triples.tile([P, ROUND], U32, align_bytes=64, name="h_codes")
+            scales = triples.tile([P, ROUND], U8, align_bytes=64, name="h_scales")
+            nc.vector.quantize_mx(
+                out=codes[:].bitcast(FP8X4),
+                scales=scales[:],
+                in_=h_grouped[r][:].rearrange("p c t -> p (c t)"),
+            )
+            h_mx[r] = (codes, scales)
+
+        def output_matmuls(r):
+            x_codes, x_scales = x_mx[r]
+            h_codes, h_scales = h_mx[r]
+            bank = result_psum.tile([P, TILES, OUTS], F32, tag="bank")
+            for j in range(TILES):
+                rows = slice(j * P, (j + 1) * P)
+                nc.tensor.matmul_mx(
+                    out=bank[:, j, :],
+                    lhsT=x_codes[:, rows].bitcast(FP8X4),
+                    lhsT_scale=x_scales[:, rows],
+                    rhs=w_codes[:, OUT_W0].bitcast(FP8X4),
+                    rhs_scale=w_scales[:, OUT_W0],
+                    start=True,
+                    stop=False,
+                )
+                nc.tensor.matmul_mx(
+                    out=bank[:, j, :],
+                    lhsT=h_codes[:, rows].bitcast(FP8X4),
+                    lhsT_scale=h_scales[:, rows],
+                    rhs=w_codes[:, W1].bitcast(FP8X4),
+                    rhs_scale=w_scales[:, W1],
+                    start=False,
+                    stop=True,
+                )
+            result_banks[r] = bank
+
+        def add_bias_and_store(r):
+            result = triples.tile([P, TILES, OUTS], F32, name="result")
+            nc.vector.tensor_tensor(
+                out=result[:],
+                in0=result_banks[r][:],
+                in1=bias_out[:].unsqueeze(1).to_broadcast([P, TILES, OUTS]),
+                op=mybir.AluOpType.add,
+            )
+            nc.sync.dma_start(
+                out=out[r * ROUND : (r + 1) * ROUND, :].rearrange("(p j) o -> p j o", j=TILES),
+                in_=result[:],
+            )
+
+        def live(r):
+            return 0 <= r < ROUNDS
+
+        transpose_x(0)
+        for s in range(ROUNDS + 3):
+            if live(s):
+                copy_x_out(s)
+            if live(s - 1):
+                relu_out(s - 1)
+            if live(s - 2):
+                regroup_h(s - 2)
+            if live(s):
+                quantise_x(s)
+            if live(s - 2):
+                quantise_h(s - 2)
+            if live(s + 1):
+                transpose_x(s + 1)
+            if live(s):
+                hidden_matmuls(s)
+            if live(s - 2):
+                output_matmuls(s - 2)
+            if live(s - 3):
+                add_bias_and_store(s - 3)

@@ -20,6 +20,7 @@ ROUND = 512
 TILES = ROUND // P
 ROUNDS = BATCH // ROUND
 W_TILES = 6
+VECTOR_HELPS = 2
 
 OUT_W0 = slice(HIDDEN, HIDDEN + OUTS)
 W1 = slice(HIDDEN + OUTS, HIDDEN + 2 * OUTS)
@@ -118,10 +119,17 @@ def tile_spn_t_kernel(tc, x, w0, w1, biases, out):
 
         def copy_x_out(r):
             grouped = pairs.tile([P, TILES, P, PACK], BF16, align_bytes=64, name="x_grouped")
-            for b, bank in enumerate(x_banks[r]):
+            first_bank, second_bank = x_banks[r]
+            nc.scalar.copy(
+                out=grouped[:, 0:2, :, :].bitcast(F32), in_=words_side_by_side(first_bank)
+            )
+            if r % VECTOR_HELPS == VECTOR_HELPS - 1:
+                nc.vector.tensor_copy(
+                    out=grouped[:, 2:4, :, :].bitcast(F32), in_=words_side_by_side(second_bank)
+                )
+            else:
                 nc.scalar.copy(
-                    out=grouped[:, 2 * b : 2 * b + 2, :, :].bitcast(F32),
-                    in_=words_side_by_side(bank),
+                    out=grouped[:, 2:4, :, :].bitcast(F32), in_=words_side_by_side(second_bank)
                 )
             x_grouped[r] = grouped
 

@@ -20,7 +20,7 @@ ROUND = 512
 TILES = ROUND // P
 ROUNDS = BATCH // ROUND
 W_TILES = 6
-VECTOR_HELPS = 2
+VECTOR_ROWS = 320
 
 OUT_W0 = slice(HIDDEN, HIDDEN + OUTS)
 W1 = slice(HIDDEN + OUTS, HIDDEN + 2 * OUTS)
@@ -45,14 +45,20 @@ def words_side_by_side(bank):
     return bank[:].rearrange("p j u r -> p j r u")
 
 
+def copy_four_tiles_out(nc, banks, grouped):
+    nc.scalar.copy(out=grouped[:, 0:2, :, :].bitcast(F32), in_=words_side_by_side(banks[0]))
+    nc.vector.tensor_copy(
+        out=grouped[:, 2:4, :, :].bitcast(F32), in_=words_side_by_side(banks[1])
+    )
+
+
 def tile_spn_t_kernel(tc, x, w0, w1, biases, out):
     nc = tc.nc
     with ExitStack() as stack:
         stack.enter_context(tc.manual_schedule())
         keep = stack.enter_context(tc.tile_pool(name="keep", bufs=1))
-        pairs = stack.enter_context(tc.tile_pool(name="pairs", bufs=2))
-        triples = stack.enter_context(tc.tile_pool(name="triples", bufs=3))
-        fours = stack.enter_context(tc.tile_pool(name="fours", bufs=4))
+        stream = stack.enter_context(tc.tile_pool(name="stream", bufs=3))
+        x_mx_pool = stack.enter_context(tc.tile_pool(name="x_mx", bufs=6))
         transposed_psum = stack.enter_context(tc.psum_pool(name="transposed", bufs=2))
         hidden_psum = stack.enter_context(tc.psum_pool(name="hidden", bufs=PACK))
         result_psum = stack.enter_context(tc.psum_pool(name="result", bufs=2))
@@ -62,16 +68,21 @@ def tile_spn_t_kernel(tc, x, w0, w1, biases, out):
             out=w_rows[:, 0:PACK, :].rearrange("m (u e) k -> m u (e k)", u=HALVES),
             in_=w0[0:HIDDEN, :].rearrange("(u m e) k -> m u (e k)", u=HALVES, e=2),
         )
-        nc.sync.dma_start(out=w_rows[:, PACK, :], in_=w0[HIDDEN : HIDDEN + OUTS, :])
-        nc.sync.dma_start(out=w_rows[:, PACK + 1, :], in_=w1[:, :])
         x_rows = []
-        for r in range(ROUNDS):
+
+        def load_x(r):
             rows = keep.tile([P, TILES, INPUTS], BF16, name="x_rows_%d" % r)
             nc.sync.dma_start(
                 out=rows[:],
                 in_=x[r * ROUND : (r + 1) * ROUND, :].rearrange("(p j) k -> p j k", j=TILES),
             )
             x_rows.append(rows)
+
+        load_x(0)
+        nc.sync.dma_start(out=w_rows[:, PACK, :], in_=w0[HIDDEN : HIDDEN + OUTS, :])
+        nc.sync.dma_start(out=w_rows[:, PACK + 1, :], in_=w1[:, :])
+        for r in range(1, ROUNDS):
+            load_x(r)
         bias_hidden = keep.tile([P, PACK], BF16)
         nc.scalar.dma_start(
             out=bias_hidden[:].rearrange("m (u e) -> m u e", u=HALVES),
@@ -88,13 +99,8 @@ def tile_spn_t_kernel(tc, x, w0, w1, biases, out):
         w_grouped = keep.tile([P, W_TILES, P, PACK], BF16, align_bytes=64)
         w_codes = keep.tile([P, W_TILES * P], U32, align_bytes=64)
         w_scales = keep.tile([P, W_TILES * P], U8, align_bytes=64)
-        for first in range(0, W_TILES, 2):
-            bank = transpose_two_tiles(nc, hidden_psum, identity, w_rows, first)
-            nc.vector.tensor_copy(
-                out=w_grouped[:, first : first + 2, :, :].bitcast(F32),
-                in_=words_side_by_side(bank),
-            )
-        for first, last in ((0, 4), (4, 6)):
+
+        def quantise_w(first, last):
             columns = slice(first * P, last * P)
             nc.vector.quantize_mx(
                 out=w_codes[:, columns].bitcast(FP8X4),
@@ -118,24 +124,13 @@ def tile_spn_t_kernel(tc, x, w0, w1, biases, out):
             ]
 
         def copy_x_out(r):
-            grouped = pairs.tile([P, TILES, P, PACK], BF16, align_bytes=64, name="x_grouped")
-            first_bank, second_bank = x_banks[r]
-            nc.scalar.copy(
-                out=grouped[:, 0:2, :, :].bitcast(F32), in_=words_side_by_side(first_bank)
-            )
-            if r % VECTOR_HELPS == VECTOR_HELPS - 1:
-                nc.vector.tensor_copy(
-                    out=grouped[:, 2:4, :, :].bitcast(F32), in_=words_side_by_side(second_bank)
-                )
-            else:
-                nc.scalar.copy(
-                    out=grouped[:, 2:4, :, :].bitcast(F32), in_=words_side_by_side(second_bank)
-                )
+            grouped = stream.tile([P, TILES, P, PACK], BF16, align_bytes=64, name="x_grouped")
+            copy_four_tiles_out(nc, x_banks[r], grouped)
             x_grouped[r] = grouped
 
         def quantise_x(r):
-            codes = fours.tile([P, ROUND], U32, align_bytes=64, name="x_codes")
-            scales = fours.tile([P, ROUND], U8, align_bytes=64, name="x_scales")
+            codes = x_mx_pool.tile([P, ROUND], U32, align_bytes=64, name="x_codes")
+            scales = x_mx_pool.tile([P, ROUND], U8, align_bytes=64, name="x_scales")
             nc.vector.quantize_mx(
                 out=codes[:].bitcast(FP8X4),
                 scales=scales[:],
@@ -161,7 +156,7 @@ def tile_spn_t_kernel(tc, x, w0, w1, biases, out):
                 h_banks[r].append(bank)
 
         def relu_out(r):
-            planes = triples.tile([P, PACK, ROUND], BF16, name="h_planes")
+            planes = stream.tile([P, PACK, ROUND], BF16, name="h_planes")
             for t, bank in enumerate(h_banks[r]):
                 nc.scalar.activation(
                     out=planes[:, t, :],
@@ -173,16 +168,25 @@ def tile_spn_t_kernel(tc, x, w0, w1, biases, out):
             h_planes[r] = planes
 
         def regroup_h(r):
-            grouped = pairs.tile([P, ROUND, PACK], BF16, align_bytes=64, name="h_grouped")
+            planes = h_planes[r]
+            grouped = stream.tile([P, ROUND, PACK], BF16, align_bytes=64, name="h_grouped")
             nc.vector.tensor_copy(
-                out=grouped[:].rearrange("p (c i) t -> p c t i", i=4),
-                in_=h_planes[r][:].rearrange("p t (c i) -> p c t i", i=4),
+                out=grouped[:, 0:VECTOR_ROWS, :].rearrange("p (c i) t -> p c t i", i=4),
+                in_=planes[:, :, 0:VECTOR_ROWS].rearrange("p t (c i) -> p c t i", i=4),
+            )
+            nc.gpsimd.tensor_scalar(
+                out=grouped[:, VECTOR_ROWS:ROUND, :],
+                in0=planes[:, :, VECTOR_ROWS:ROUND].rearrange("p t c -> p c t"),
+                scalar1=1.0,
+                scalar2=0.0,
+                op0=mybir.AluOpType.mult,
+                op1=mybir.AluOpType.add,
             )
             h_grouped[r] = grouped
 
         def quantise_h(r):
-            codes = triples.tile([P, ROUND], U32, align_bytes=64, name="h_codes")
-            scales = triples.tile([P, ROUND], U8, align_bytes=64, name="h_scales")
+            codes = stream.tile([P, ROUND], U32, align_bytes=64, name="h_codes")
+            scales = stream.tile([P, ROUND], U8, align_bytes=64, name="h_scales")
             nc.vector.quantize_mx(
                 out=codes[:].bitcast(FP8X4),
                 scales=scales[:],
@@ -217,7 +221,7 @@ def tile_spn_t_kernel(tc, x, w0, w1, biases, out):
             result_banks[r] = bank
 
         def add_bias_and_store(r):
-            result = triples.tile([P, TILES, OUTS], F32, name="result")
+            result = stream.tile([P, TILES, OUTS], F32, name="result")
             nc.vector.tensor_tensor(
                 out=result[:],
                 in0=result_banks[r][:],
@@ -232,23 +236,40 @@ def tile_spn_t_kernel(tc, x, w0, w1, biases, out):
         def live(r):
             return 0 <= r < ROUNDS
 
+        hidden_w_banks = [
+            transpose_two_tiles(nc, hidden_psum, identity, w_rows, first)
+            for first in range(0, PACK, 2)
+        ]
         transpose_x(0)
-        for s in range(ROUNDS + 3):
+        output_w_bank = transpose_two_tiles(nc, result_psum, identity, w_rows, PACK)
+        copy_four_tiles_out(nc, hidden_w_banks, w_grouped[:, 0:PACK, :, :])
+        copy_x_out(0)
+        quantise_w(0, PACK)
+        quantise_x(0)
+        nc.scalar.copy(
+            out=w_grouped[:, PACK:W_TILES, :, :].bitcast(F32),
+            in_=words_side_by_side(output_w_bank),
+        )
+        quantise_w(PACK, W_TILES)
+        transpose_x(1)
+        hidden_matmuls(0)
+
+        for s in range(1, ROUNDS + 4):
             if live(s):
                 copy_x_out(s)
             if live(s - 1):
                 relu_out(s - 1)
-            if live(s - 2):
-                regroup_h(s - 2)
+            if live(s - 3):
+                quantise_h(s - 3)
             if live(s):
                 quantise_x(s)
             if live(s - 2):
-                quantise_h(s - 2)
+                regroup_h(s - 2)
+            if live(s - 4):
+                output_matmuls(s - 4)
             if live(s + 1):
                 transpose_x(s + 1)
             if live(s):
                 hidden_matmuls(s)
-            if live(s - 2):
-                output_matmuls(s - 2)
-            if live(s - 3):
-                add_bias_and_store(s - 3)
+            if live(s - 4):
+                add_bias_and_store(s - 4)

from contextlib import ExitStack

import concourse.mybir as mybir
from concourse.masks import make_identity

BF16 = mybir.dt.bfloat16
F32 = mybir.dt.float32
U32 = mybir.dt.uint32
U8 = mybir.dt.uint8
FP8X4 = mybir.dt.float8_e4m3fn_x4

P = 128
PACK = 4
HALVES = 2
BATCH = 8192
INPUTS = 512
HIDDEN = 512
OUTS = 128
ROUND = 512
TILES = ROUND // P
ROUNDS = BATCH // ROUND
W_TILES = 6
VECTOR_ROWS = 320

OUT_W0 = slice(HIDDEN, HIDDEN + OUTS)
W1 = slice(HIDDEN + OUTS, HIDDEN + 2 * OUTS)

FLOPS = 2 * BATCH * INPUTS * (HIDDEN + OUTS) + 2 * BATCH * HIDDEN * OUTS


def transpose_two_tiles(nc, banks, identity, rows, first):
    bank = banks.tile([P, 2, HALVES, P], F32, tag="bank")
    for j in range(2):
        words = rows[:, first + j, :].bitcast(F32)
        for u in range(HALVES):
            nc.tensor.transpose(
                out=bank[:, j, u, :],
                in_=words[:, u * P : (u + 1) * P],
                identity=identity[:],
            )
    return bank


def words_side_by_side(bank):
    return bank[:].rearrange("p j u r -> p j r u")


def copy_four_tiles_out(nc, banks, grouped):
    nc.scalar.copy(out=grouped[:, 0:2, :, :].bitcast(F32), in_=words_side_by_side(banks[0]))
    nc.vector.tensor_copy(
        out=grouped[:, 2:4, :, :].bitcast(F32), in_=words_side_by_side(banks[1])
    )


def tile_spn_t_kernel(tc, x, w0, w1, biases, out):
    nc = tc.nc
    with ExitStack() as stack:
        stack.enter_context(tc.manual_schedule())
        keep = stack.enter_context(tc.tile_pool(name="keep", bufs=1))
        stream = stack.enter_context(tc.tile_pool(name="stream", bufs=3))
        x_mx_pool = stack.enter_context(tc.tile_pool(name="x_mx", bufs=6))
        transposed_psum = stack.enter_context(tc.psum_pool(name="transposed", bufs=2))
        hidden_psum = stack.enter_context(tc.psum_pool(name="hidden", bufs=PACK))
        result_psum = stack.enter_context(tc.psum_pool(name="result", bufs=2))

        w_rows = keep.tile([P, W_TILES, INPUTS], BF16)
        nc.sync.dma_start(
            out=w_rows[:, 0:PACK, :].rearrange("m (u e) k -> m u (e k)", u=HALVES),
            in_=w0[0:HIDDEN, :].rearrange("(u m e) k -> m u (e k)", u=HALVES, e=2),
        )
        x_rows = []

        def load_x(r):
            rows = keep.tile([P, TILES, INPUTS], BF16, name="x_rows_%d" % r)
            nc.sync.dma_start(
                out=rows[:],
                in_=x[r * ROUND : (r + 1) * ROUND, :].rearrange("(p j) k -> p j k", j=TILES),
            )
            x_rows.append(rows)

        load_x(0)
        nc.sync.dma_start(out=w_rows[:, PACK, :], in_=w0[HIDDEN : HIDDEN + OUTS, :])
        nc.sync.dma_start(out=w_rows[:, PACK + 1, :], in_=w1[:, :])
        for r in range(1, ROUNDS):
            load_x(r)
        bias_hidden = keep.tile([P, PACK], BF16)
        nc.scalar.dma_start(
            out=bias_hidden[:].rearrange("m (u e) -> m u e", u=HALVES),
            in_=biases[0:HIDDEN].rearrange("(u m e) -> m u e", u=HALVES, e=2),
        )
        bias_out = keep.tile([P, OUTS], BF16)
        nc.scalar.dma_start(
            out=bias_out[:], in_=biases[HIDDEN : HIDDEN + OUTS].partition_broadcast(P)
        )

        identity = keep.tile([P, P], F32)
        make_identity(nc, identity[:])

        w_grouped = keep.tile([P, W_TILES, P, PACK], BF16, align_bytes=64)
        w_codes = keep.tile([P, W_TILES * P], U32, align_bytes=64)
        w_scales = keep.tile([P, W_TILES * P], U8, align_bytes=64)

        def quantise_w(first, last):
            columns = slice(first * P, last * P)
            nc.vector.quantize_mx(
                out=w_codes[:, columns].bitcast(FP8X4),
                scales=w_scales[:, columns],
                in_=w_grouped[:, first:last, :, :].rearrange("p j r t -> p (j r t)"),
            )

        x_banks = {}
        x_grouped = {}
        x_mx = {}
        h_banks = {}
        h_planes = {}
        h_grouped = {}
        h_mx = {}
        result_banks = {}

        def transpose_x(r):
            x_banks[r] = [
                transpose_two_tiles(nc, transposed_psum, identity, x_rows[r], first)
                for first in range(0, TILES, 2)
            ]

        def copy_x_out(r):
            grouped = stream.tile([P, TILES, P, PACK], BF16, align_bytes=64, name="x_grouped")
            copy_four_tiles_out(nc, x_banks[r], grouped)
            x_grouped[r] = grouped

        def quantise_x(r):
            codes = x_mx_pool.tile([P, ROUND], U32, align_bytes=64, name="x_codes")
            scales = x_mx_pool.tile([P, ROUND], U8, align_bytes=64, name="x_scales")
            nc.vector.quantize_mx(
                out=codes[:].bitcast(FP8X4),
                scales=scales[:],
                in_=x_grouped[r][:].rearrange("p j r t -> p (j r t)"),
            )
            x_mx[r] = (codes, scales)

        def hidden_matmuls(r):
            codes, scales = x_mx[r]
            h_banks[r] = []
            for t in range(PACK):
                nodes = slice(t * P, (t + 1) * P)
                bank = hidden_psum.tile([P, ROUND], F32, tag="bank")
                nc.tensor.matmul_mx(
                    out=bank[:],
                    lhsT=w_codes[:, nodes].bitcast(FP8X4),
                    lhsT_scale=w_scales[:, nodes],
                    rhs=codes[:].bitcast(FP8X4),
                    rhs_scale=scales[:],
                    start=True,
                    stop=True,
                )
                h_banks[r].append(bank)

        def relu_out(r):
            planes = stream.tile([P, PACK, ROUND], BF16, name="h_planes")
            for t, bank in enumerate(h_banks[r]):
                nc.scalar.activation(
                    out=planes[:, t, :],
                    in_=bank[:],
                    func=mybir.ActivationFunctionType.Relu,
                    bias=bias_hidden[:, t : t + 1],
                    scale=1.0,
                )
            h_planes[r] = planes

        def regroup_h(r):
            planes = h_planes[r]
            grouped = stream.tile([P, ROUND, PACK], BF16, align_bytes=64, name="h_grouped")
            nc.vector.tensor_copy(
                out=grouped[:, 0:VECTOR_ROWS, :].rearrange("p (c i) t -> p c t i", i=4),
                in_=planes[:, :, 0:VECTOR_ROWS].rearrange("p t (c i) -> p c t i", i=4),
            )
            nc.gpsimd.tensor_scalar(
                out=grouped[:, VECTOR_ROWS:ROUND, :],
                in0=planes[:, :, VECTOR_ROWS:ROUND].rearrange("p t c -> p c t"),
                scalar1=1.0,
                scalar2=0.0,
                op0=mybir.AluOpType.mult,
                op1=mybir.AluOpType.add,
            )
            h_grouped[r] = grouped

        def quantise_h(r):
            codes = stream.tile([P, ROUND], U32, align_bytes=64, name="h_codes")
            scales = stream.tile([P, ROUND], U8, align_bytes=64, name="h_scales")
            nc.vector.quantize_mx(
                out=codes[:].bitcast(FP8X4),
                scales=scales[:],
                in_=h_grouped[r][:].rearrange("p c t -> p (c t)"),
            )
            h_mx[r] = (codes, scales)

        def output_matmuls(r):
            x_codes, x_scales = x_mx[r]
            h_codes, h_scales = h_mx[r]
            bank = result_psum.tile([P, TILES, OUTS], F32, tag="bank")
            for j in range(TILES):
                rows = slice(j * P, (j + 1) * P)
                nc.tensor.matmul_mx(
                    out=bank[:, j, :],
                    lhsT=x_codes[:, rows].bitcast(FP8X4),
                    lhsT_scale=x_scales[:, rows],
                    rhs=w_codes[:, OUT_W0].bitcast(FP8X4),
                    rhs_scale=w_scales[:, OUT_W0],
                    start=True,
                    stop=False,
                )
                nc.tensor.matmul_mx(
                    out=bank[:, j, :],
                    lhsT=h_codes[:, rows].bitcast(FP8X4),
                    lhsT_scale=h_scales[:, rows],
                    rhs=w_codes[:, W1].bitcast(FP8X4),
                    rhs_scale=w_scales[:, W1],
                    start=False,
                    stop=True,
                )
            result_banks[r] = bank

        def add_bias_and_store(r):
            result = stream.tile([P, TILES, OUTS], F32, name="result")
            nc.vector.tensor_tensor(
                out=result[:],
                in0=result_banks[r][:],
                in1=bias_out[:].unsqueeze(1).to_broadcast([P, TILES, OUTS]),
                op=mybir.AluOpType.add,
            )
            nc.sync.dma_start(
                out=out[r * ROUND : (r + 1) * ROUND, :].rearrange("(p j) o -> p j o", j=TILES),
                in_=result[:],
            )

        def live(r):
            return 0 <= r < ROUNDS

        hidden_w_banks = [
            transpose_two_tiles(nc, hidden_psum, identity, w_rows, first)
            for first in range(0, PACK, 2)
        ]
        transpose_x(0)
        output_w_bank = transpose_two_tiles(nc, result_psum, identity, w_rows, PACK)
        copy_four_tiles_out(nc, hidden_w_banks, w_grouped[:, 0:PACK, :, :])
        copy_x_out(0)
        quantise_w(0, PACK)
        quantise_x(0)
        nc.scalar.copy(
            out=w_grouped[:, PACK:W_TILES, :, :].bitcast(F32),
            in_=words_side_by_side(output_w_bank),
        )
        quantise_w(PACK, W_TILES)
        transpose_x(1)
        hidden_matmuls(0)

        for s in range(1, ROUNDS + 4):
            if live(s):
                copy_x_out(s)
            if live(s - 1):
                relu_out(s - 1)
            if live(s - 3):
                quantise_h(s - 3)
            if live(s):
                quantise_x(s)
            if live(s - 2):
                regroup_h(s - 2)
            if live(s - 4):
                output_matmuls(s - 4)
            if live(s + 1):
                transpose_x(s + 1)
            if live(s):
                hidden_matmuls(s)
            if live(s - 4):
                add_bias_and_store(s - 4)
